import numpy as np
import ml_dtypes


def mxq(x, axis, fmt="e4m3"):
    dtype, down = {"e4m3": (ml_dtypes.float8_e4m3fn, 7), "e5m2": (ml_dtypes.float8_e5m2, 14)}[fmt]
    v = np.moveaxis(np.asarray(x, np.float32).astype(ml_dtypes.bfloat16).astype(np.float64), axis, -1)
    blocks = v.reshape(v.shape[:-1] + (-1, 32))
    amax = np.abs(blocks).max(-1, keepdims=True)
    byte = np.maximum(np.where(amax > 0, np.frexp(amax)[1] - 1 + 127, 0) - down, 1)
    scale = np.exp2(byte - 127.0)
    codes = (blocks / scale).astype(np.float32).astype(dtype).astype(np.float64)
    return np.moveaxis((codes * scale).reshape(v.shape), -1, axis)


WIDE = False


def mx_kscale(k):
    if not WIDE:
        return np.ones(k)
    levels = np.array([10, -10, 5, -5, 0])
    a = np.random.permutation(np.resize(levels, k // 512 * 4)).reshape(k // 512, 4)
    idx = np.arange(k)
    return np.exp2(a[idx // 512, idx % 128 // 32])


BF16 = ml_dtypes.bfloat16


def bf(x):
    return np.asarray(x, np.float32).astype(BF16)


def f64(x):
    return np.asarray(x).astype(np.float64)


E2M1 = np.array([0.0, 0.5, 1.0, 1.5, 2.0, 3.0, 4.0, 6.0, -0.0, -0.5, -1.0, -1.5, -2.0, -3.0, -4.0, -6.0])


def pack_weight(w, fmt):
    k, n = w.shape
    w = f64(bf(w)).reshape(k // 32, 32, n)
    amax = np.abs(w).max(1)
    if fmt == "e4m3":
        byte = np.frexp(amax)[1] - 1 + 127 - 7
    else:
        mant, ex = np.frexp(amax / 6.0)
        byte = np.where(mant > 0.5, ex, ex - 1) + 127
    byte = np.clip(np.where(amax > 0, byte, 1), 1, 254)
    scaled = (w * np.exp2(127.0 - byte)[:, None, :]).reshape(k, n).astype(np.float32)
    by_word = np.ascontiguousarray(scaled.reshape(k // 512, 128, 4, n).transpose(0, 1, 3, 2))
    if fmt == "e4m3":
        words = by_word.astype(ml_dtypes.float8_e4m3fn).view(np.uint8)
    else:
        c = by_word.astype(ml_dtypes.float4_e2m1fn).view(np.uint8) & 0xF
        words = c[..., 0::2] | (c[..., 1::2] << 4)
    return np.ascontiguousarray(words), np.ascontiguousarray(byte.astype(np.uint8).reshape(k // 512, 16, n))


def unpack_weight(words, scales, fmt):
    g, p, n, _ = words.shape
    if fmt == "e4m3":
        vals = np.ascontiguousarray(words).view(ml_dtypes.float8_e4m3fn).astype(np.float64)
    else:
        nib = np.empty((g, p, n, 4), np.uint8)
        nib[..., 0::2] = words & 0xF
        nib[..., 1::2] = words >> 4
        vals = E2M1[nib]
    vals = vals * np.repeat(np.exp2(scales.astype(np.float64) - 127.0), 8, axis=1)[..., None]
    return vals.transpose(0, 1, 3, 2).reshape(g * 512, n)


B, T, DX, DY, F = 128, 8, 1024, 1024, 5
MIN_CONTEXT = 1
G = 1.5 / DY ** 0.25


def setup_inputs():
    s, t = mx_kscale(DX), mx_kscale(DY)
    embeddings = bf(np.random.standard_normal((B, T, DX)) * s)
    contexts = bf(np.random.standard_normal((B, T, DY)) * G / t)
    stack = (np.random.standard_normal((F, DY, DX)) * G / np.sqrt(DX) * t[:, None] / s).swapaxes(1, 2)
    words, scales = pack_weight(stack.reshape(-1, DY), "e4m3")
    return {"embeddings": embeddings,
            "contexts": contexts,
            "W_words": words,
            "W_scales": scales}


def reference(embeddings, contexts, W_words, W_scales):
    eq = mxq(f64(embeddings)[:, MIN_CONTEXT:T], 2, "e4m3")
    cq = mxq(f64(contexts)[:, MIN_CONTEXT - 1:T - 1], 2, "e4m3")
    wq = unpack_weight(W_words, W_scales, "e4m3").reshape(F, DX, DY)
    losses = []
    for step in range(F):
        S = T - step - MIN_CONTEXT
        xw = eq[:, step:] @ wq[step]
        scores = mxq(xw, 2, "e4m3").transpose(1, 0, 2) @ cq[:, :S].transpose(1, 2, 0)
        pos = np.diagonal(scores, axis1=1, axis2=2)
        m = scores.max(2, keepdims=True)
        lse = np.log(np.exp(scores - m).sum(2)) + m[:, :, 0] - np.log(B * S)
        losses.append((lse - pos).T.reshape(-1))
    return np.concatenate(losses)

@@ -1,0 +1,334 @@
+import math
+from contextlib import ExitStack
+
+import concourse.mybir as mybir
+from concourse.masks import make_identity
+
+F32 = mybir.dt.float32
+BF16 = mybir.dt.bfloat16
+I32 = mybir.dt.int32
+U32 = mybir.dt.uint32
+U8 = mybir.dt.uint8
+FP8X4 = mybir.dt.float8_e4m3fn_x4
+ALU = mybir.AluOpType
+ACT = mybir.ActivationFunctionType
+AXIS_X = mybir.AxisListType.X
+
+P = 128
+T = 8
+D = 1024
+STEPS = 5
+PACK = 4
+K_PASS = P * PACK
+PASSES = D // K_PASS
+PLANES_PER_TILE = 4
+QUADRANT = 32
+ROWS_PER_GROUP = 8
+GROUPS = P // ROWS_PER_GROUP
+QUANTISE_LAG = 1
+COMPARE_LAG = 3
+EXP_LAG = 4
+
+N_PAIRS = sum(T - 1 - step for step in range(STEPS))
+FLOPS = 2 * N_PAIRS * P * D * D + 2 * N_PAIRS * P * P * D
+
+
+def times_of(step):
+    return T - 1 - step
+
+
+def first_column(step):
+    return sum(times_of(k) for k in range(step))
+
+
+def tile_infonceloss_pa_e_kernel(tc, embeddings, contexts, W_words, W_scales, out):
+    nc = tc.nc
+    step_order = list(reversed(range(STEPS)))
+    first_step, second_step = step_order[0], step_order[1]
+    pairs = [(step, s) for step in step_order for s in range(times_of(step))]
+
+    with ExitStack() as ctx:
+        keep = ctx.enter_context(tc.tile_pool(name="keep", bufs=1))
+        slice_stage = ctx.enter_context(tc.tile_pool(name="slice_stage", bufs=4))
+        xw_stage = ctx.enter_context(tc.tile_pool(name="xw_stage", bufs=3))
+        unread = ctx.enter_context(tc.tile_pool(name="unread", bufs=4))
+        psum_xw = ctx.enter_context(tc.psum_pool(name="psum_xw", bufs=4))
+        psum_scores = ctx.enter_context(tc.psum_pool(name="psum_scores", bufs=2))
+        psum_turned = ctx.enter_context(tc.psum_pool(name="psum_turned", bufs=2))
+        ctx.enter_context(tc.manual_schedule())
+
+        e_raw = keep.tile([P, T - 1, D], BF16)
+        c_raw = keep.tile([P, T - 1, D], BF16)
+        w_words = keep.tile([P, STEPS, PASSES, D], U32, align_bytes=64)
+        n_planes = STEPS * PASSES
+        n_slots = (n_planes + PLANES_PER_TILE - 1) // PLANES_PER_TILE
+        w_planes = keep.tile([P, n_slots, D], U8, align_bytes=64)
+        e_words = keep.tile([P, T - 1, PASSES, P], U32, align_bytes=64)
+        e_scales = keep.tile([P, T - 1, PASSES, P], U8, align_bytes=64)
+        c_words = keep.tile([P, T - 1, PASSES, P], U32, align_bytes=64)
+        c_scales = keep.tile([P, T - 1, PASSES, P], U8, align_bytes=64)
+        xw_words = keep.tile([P, N_PAIRS, PASSES, P], U32, align_bytes=64)
+        xw_scales = keep.tile([P, N_PAIRS, PASSES, P], U8, align_bytes=64)
+        neg_max = keep.tile([P, N_PAIRS], F32)
+        sum_exp = keep.tile([P, N_PAIRS], F32)
+        diagonal = keep.tile([P, N_PAIRS], F32)
+        shift = keep.tile([P, N_PAIRS], F32)
+        spread_sum = keep.tile([P, ROWS_PER_GROUP * N_PAIRS], F32)
+        spread_shift = keep.tile([P, ROWS_PER_GROUP * N_PAIRS], F32)
+
+        nc.vector.memset(w_planes[:].bitcast(I32), 0)
+
+        def load_embeddings(lo, hi):
+            nc.sync.dma_start(out=e_raw[:, lo - 1 : hi - 1, :], in_=embeddings[:, lo:hi, :])
+
+        def load_contexts(lo, hi):
+            nc.sync.dma_start(out=c_raw[:, lo:hi, :], in_=contexts[:, lo:hi, :])
+
+        def load_weight(step):
+            nc.sync.dma_start(
+                out=w_words[:, step, :, :].bitcast(I32),
+                in_=W_words[PASSES * step : PASSES * (step + 1)]
+                .rearrange("g p n t -> p g (n t)")
+                .bitcast(I32),
+            )
+
+        def load_scale_slot(slot):
+            lo = PLANES_PER_TILE * slot
+            hi = min(lo + PLANES_PER_TILE, n_planes)
+            for quadrant in range(P // QUADRANT):
+                top = QUADRANT * quadrant
+                nc.sync.dma_start(
+                    out=w_planes[top : top + 4 * (hi - lo), slot, :].bitcast(I32),
+                    in_=W_scales[lo:hi, 4 * quadrant : 4 * quadrant + 4, :].bitcast(I32),
+                )
+
+        load_embeddings(1 + second_step, T)
+        load_scale_slot(PASSES * first_step // PLANES_PER_TILE)
+        load_weight(first_step)
+        load_contexts(0, times_of(first_step))
+        for slot in reversed(range(PASSES * first_step // PLANES_PER_TILE)):
+            load_scale_slot(slot)
+        load_weight(second_step)
+        load_contexts(times_of(first_step), T - 1)
+        load_embeddings(1, 1 + second_step)
+        for step in step_order[2:]:
+            load_weight(step)
+
+        ident_f32 = keep.tile([P, P], F32)
+        make_identity(nc, ident_f32[:])
+        ident_bf16 = keep.tile([P, P], BF16)
+        make_identity(nc, ident_bf16[:])
+        group_of_row = keep.tile([P, P], F32)
+        nc.vector.memset(group_of_row[:], 0.0)
+        nc.vector.tensor_reduce(
+            out=group_of_row[:, 0:GROUPS],
+            in_=ident_f32[:].rearrange("p (q i) -> p q i", i=ROWS_PER_GROUP),
+            axis=AXIS_X,
+            op=ALU.add,
+        )
+        place_in_group = keep.tile([P, ROWS_PER_GROUP], F32)
+        nc.vector.tensor_reduce(
+            out=place_in_group[:],
+            in_=ident_f32[:].rearrange("p (q i) -> p i q", i=ROWS_PER_GROUP),
+            axis=AXIS_X,
+            op=ALU.add,
+        )
+
+        def turn_embedding_slice(te):
+            pairs_of_d = e_raw[:, te - 1, :].bitcast(F32)
+            words_per_pass = K_PASS // 2
+            turned = psum_turned.tile([P, PASSES, 2, P], F32, tag="turned")
+            for g in range(PASSES):
+                for u in range(2):
+                    nc.tensor.transpose(
+                        turned[:, g, u, :],
+                        pairs_of_d[:, words_per_pass * g + u : words_per_pass * (g + 1) : 2],
+                        ident_f32[:],
+                    )
+            grouped = slice_stage.tile([P, PASSES, P, PACK], BF16, tag="grouped", align_bytes=64)
+            nc.scalar.copy(out=grouped[:].bitcast(F32), in_=turned[:].rearrange("p g u b -> p g b u"))
+            return grouped
+
+        def turn_context_slice(s):
+            grouped = slice_stage.tile([P, PASSES, P, PACK], BF16, tag="grouped", align_bytes=64)
+            for g in range(PASSES):
+                turned = psum_turned.tile([P, PACK, P], BF16, tag="turned")
+                for t in range(PACK):
+                    lo = K_PASS * g + P * t
+                    nc.tensor.transpose(turned[:, t, :], c_raw[:, s, lo : lo + P], ident_bf16[:])
+                copy_out = nc.scalar.copy if g == 0 else nc.vector.tensor_copy
+                copy_out(out=grouped[:, g, :, :], in_=turned[:].rearrange("p t j -> p j t"))
+            return grouped
+
+        def quantise(grouped, words, scales):
+            nc.vector.quantize_mx(
+                out=words.rearrange("p g b -> p (g b)").bitcast(FP8X4),
+                scales=scales.rearrange("p g b -> p (g b)"),
+                in_=grouped[:].rearrange("p g b t -> p (g b t)"),
+            )
+
+        def quantise_embedding_slice(te, grouped):
+            quantise(grouped, e_words[:, te - 1, :, :], e_scales[:, te - 1, :, :])
+
+        def quantise_context_slice(s, grouped):
+            quantise(grouped, c_words[:, s, :, :], c_scales[:, s, :, :])
+
+        def project(i):
+            step, s = pairs[i]
+            te = 1 + step + s
+            grouped = xw_stage.tile([P, PASSES, P, PACK], BF16, tag="xw_grouped", align_bytes=64)
+            for g in range(PASSES):
+                bank = psum_xw.tile([P, PACK, P], F32, tag="xw_bank")
+                for t in range(PACK):
+                    lo = K_PASS * g + P * t
+                    for k_pass in range(PASSES):
+                        plane = PASSES * step + k_pass
+                        slot, place = divmod(plane, PLANES_PER_TILE)
+                        nc.tensor.matmul_mx(
+                            out=bank[:, t, :],
+                            lhsT=w_words[:, step, k_pass, lo : lo + P].bitcast(FP8X4),
+                            lhsT_scale=w_planes[4 * place : P, slot, lo : lo + P],
+                            rhs=e_words[:, te - 1, k_pass, :].bitcast(FP8X4),
+                            rhs_scale=e_scales[:, te - 1, k_pass, :],
+                            start=(k_pass == 0),
+                            stop=(k_pass == PASSES - 1),
+                        )
+                to_vector = i % 2 == 1 and g == PASSES - 1
+                copy_out = nc.vector.tensor_copy if to_vector else nc.scalar.copy
+                copy_out(out=grouped[:, g, :, :], in_=bank[:].rearrange("p t b -> p b t"))
+            return grouped
+
+        def compare(i):
+            step, s = pairs[i]
+            column = first_column(step) + s
+            scores = psum_scores.tile([P, P], F32, tag="scores")
+            for g in range(PASSES):
+                nc.tensor.matmul_mx(
+                    out=scores[:],
+                    lhsT=xw_words[:, i, g, :].bitcast(FP8X4),
+                    lhsT_scale=xw_scales[:, i, g, :],
+                    rhs=c_words[:, s, g, :].bitcast(FP8X4),
+                    rhs_scale=c_scales[:, s, g, :],
+                    start=(g == 0),
+                    stop=(g == PASSES - 1),
+                )
+            nc.vector.tensor_reduce(
+                out=neg_max[:, column : column + 1], in_=scores[:], axis=AXIS_X, op=ALU.max, negate=True
+            )
+            return scores
+
+        def sum_exponentials(i, scores):
+            step, s = pairs[i]
+            column = first_column(step) + s
+            exponentials = unread.tile([P, P], F32, tag="exponentials")
+            nc.scalar.activation(
+                out=exponentials[:],
+                in_=scores[:],
+                func=ACT.Exp,
+                bias=neg_max[:, column : column + 1],
+                scale=1.0,
+                accum_out=sum_exp[:, column : column + 1],
+            )
+
+        def take_diagonal(i, scores):
+            step, s = pairs[i]
+            column = first_column(step) + s
+            masked = unread.tile([P, P], F32, tag="masked")
+            nc.vector.scalar_tensor_tensor(
+                out=masked[:],
+                in0=scores[:],
+                scalar=1.0,
+                in1=ident_f32[:],
+                op0=ALU.mult,
+                op1=ALU.mult,
+                accum_out=diagonal[:, column : column + 1],
+            )
+
+        def spread(step, values, spread_tile):
+            n_times = times_of(step)
+            lo = first_column(step)
+            shape = [P, ROWS_PER_GROUP, n_times]
+            nc.vector.tensor_tensor(
+                out=spread_tile[:, ROWS_PER_GROUP * lo : ROWS_PER_GROUP * (lo + n_times)].rearrange(
+                    "p (i s) -> p i s", s=n_times
+                ),
+                in0=values[:, lo : lo + n_times].unsqueeze(1).to_broadcast(shape),
+                in1=place_in_group[:].unsqueeze(2).to_broadcast(shape),
+                op=ALU.mult,
+            )
+
+        def spread_shift_of(step):
+            n_times = times_of(step)
+            lo = first_column(step)
+            nc.vector.scalar_tensor_tensor(
+                out=shift[:, lo : lo + n_times],
+                in0=neg_max[:, lo : lo + n_times],
+                scalar=math.log(P * n_times),
+                in1=diagonal[:, lo : lo + n_times],
+                op0=ALU.add,
+                op1=ALU.add,
+            )
+            spread(step, shift, spread_shift)
+
+        early_times = list(range(1 + second_step, T))
+        early_grouped = [turn_embedding_slice(te) for te in early_times]
+        for te, grouped in zip(early_times, early_grouped):
+            quantise_embedding_slice(te, grouped)
+        later_slices = [("contexts", s) for s in range(times_of(first_step))]
+        for step in step_order[1:]:
+            later_slices.append(("contexts", times_of(step) - 1))
+            if step >= 1:
+                later_slices.append(("embeddings", step))
+
+        def ends_step(i):
+            step, s = pairs[i]
+            return s == times_of(step) - 1
+
+        grouped_of = {}
+        scores_of = {}
+        for i in range(N_PAIRS + EXP_LAG):
+            if 0 <= i - EXP_LAG:
+                sum_exponentials(i - EXP_LAG, scores_of[i - EXP_LAG])
+                if ends_step(i - EXP_LAG):
+                    spread(pairs[i - EXP_LAG][0], sum_exp, spread_sum)
+            turns_slice = 1 <= i <= len(later_slices)
+            if turns_slice:
+                kind, time = later_slices[i - 1]
+                if kind == "contexts":
+                    slice_grouped = turn_context_slice(time)
+                else:
+                    slice_grouped = turn_embedding_slice(time)
+            if 0 <= i - COMPARE_LAG < N_PAIRS:
+                scores_of[i - COMPARE_LAG] = compare(i - COMPARE_LAG)
+                take_diagonal(i - COMPARE_LAG, scores_of[i - COMPARE_LAG])
+                if ends_step(i - COMPARE_LAG):
+                    spread_shift_of(pairs[i - COMPARE_LAG][0])
+            if 0 <= i - QUANTISE_LAG < N_PAIRS:
+                quantise(
+                    grouped_of[i - QUANTISE_LAG],
+                    xw_words[:, i - QUANTISE_LAG, :, :],
+                    xw_scales[:, i - QUANTISE_LAG, :, :],
+                )
+            if turns_slice:
+                if kind == "contexts":
+                    quantise_context_slice(time, slice_grouped)
+                else:
+                    quantise_embedding_slice(time, slice_grouped)
+            if i < N_PAIRS:
+                grouped_of[i] = project(i)
+
+        gathered_sum = psum_turned.tile([P, ROWS_PER_GROUP * N_PAIRS], F32, tag="turned")
+        nc.tensor.matmul(out=gathered_sum[:], lhsT=group_of_row[:], rhs=spread_sum[:], start=True, stop=True)
+        gathered_shift = psum_turned.tile([P, ROWS_PER_GROUP * N_PAIRS], F32, tag="turned")
+        nc.tensor.matmul(out=gathered_shift[:], lhsT=group_of_row[:], rhs=spread_shift[:], start=True, stop=True)
+        log_sum = keep.tile([GROUPS, ROWS_PER_GROUP * N_PAIRS], F32)
+        nc.scalar.activation(out=log_sum[:], in_=gathered_sum[0:GROUPS, :], func=ACT.Ln)
+        loss = keep.tile([GROUPS, ROWS_PER_GROUP * N_PAIRS], F32)
+        nc.vector.tensor_tensor(out=loss[:], in0=log_sum[:], in1=gathered_shift[0:GROUPS, :], op=ALU.subtract)
+        for step in range(STEPS):
+            lo = first_column(step)
+            hi = lo + times_of(step)
+            nc.sync.dma_start(
+                out=out[P * lo : P * hi].rearrange("(q r) -> q r", q=GROUPS),
+                in_=loss[:, ROWS_PER_GROUP * lo : ROWS_PER_GROUP * hi],
+            )

@@ -16,57 +16,49 @@ AXIS_X = mybir.AxisListType.X
 
 P = 128
 T = 8
+N_SLICES = T - 1
 D = 1024
 STEPS = 5
 PACK = 4
 K_PASS = P * PACK
 PASSES = D // K_PASS
-PLANES_PER_TILE = 4
+PLANES_PER_SLOT = 4
 QUADRANT = 32
+SLICES_PER_LOAD = 2
 ROWS_PER_GROUP = 8
 GROUPS = P // ROWS_PER_GROUP
 QUANTISE_LAG = 1
 COMPARE_LAG = 3
 EXP_LAG = 4
 
-N_PAIRS = sum(T - 1 - step for step in range(STEPS))
+N_PAIRS = sum(N_SLICES - step for step in range(STEPS))
 FLOPS = 2 * N_PAIRS * P * D * D + 2 * N_PAIRS * P * P * D
-
-
-def times_of(step):
-    return T - 1 - step
-
-
-def first_column(step):
-    return sum(times_of(k) for k in range(step))
 
 
 def tile_infonceloss_pa_e_kernel(tc, embeddings, contexts, W_words, W_scales, out):
     nc = tc.nc
-    step_order = list(reversed(range(STEPS)))
-    first_step, second_step = step_order[0], step_order[1]
-    pairs = [(step, s) for step in step_order for s in range(times_of(step))]
+    pairs = [(step, s) for step in range(STEPS) for s in range(N_SLICES - step)]
+    first_pair = [pairs.index((step, 0)) for step in range(STEPS)]
 
     with ExitStack() as ctx:
         keep = ctx.enter_context(tc.tile_pool(name="keep", bufs=1))
         slice_stage = ctx.enter_context(tc.tile_pool(name="slice_stage", bufs=4))
         xw_stage = ctx.enter_context(tc.tile_pool(name="xw_stage", bufs=3))
         unread = ctx.enter_context(tc.tile_pool(name="unread", bufs=4))
-        psum_xw = ctx.enter_context(tc.psum_pool(name="psum_xw", bufs=4))
+        psum_banks = ctx.enter_context(tc.psum_pool(name="psum_banks", bufs=6))
         psum_scores = ctx.enter_context(tc.psum_pool(name="psum_scores", bufs=2))
-        psum_turned = ctx.enter_context(tc.psum_pool(name="psum_turned", bufs=2))
         ctx.enter_context(tc.manual_schedule())
 
-        e_raw = keep.tile([P, T - 1, D], BF16)
-        c_raw = keep.tile([P, T - 1, D], BF16)
+        e_raw = keep.tile([P, N_SLICES, D], BF16)
+        c_raw = keep.tile([P, N_SLICES, D], BF16)
         w_words = keep.tile([P, STEPS, PASSES, D], U32, align_bytes=64)
         n_planes = STEPS * PASSES
-        n_slots = (n_planes + PLANES_PER_TILE - 1) // PLANES_PER_TILE
+        n_slots = (n_planes + PLANES_PER_SLOT - 1) // PLANES_PER_SLOT
         w_planes = keep.tile([P, n_slots, D], U8, align_bytes=64)
-        e_words = keep.tile([P, T - 1, PASSES, P], U32, align_bytes=64)
-        e_scales = keep.tile([P, T - 1, PASSES, P], U8, align_bytes=64)
-        c_words = keep.tile([P, T - 1, PASSES, P], U32, align_bytes=64)
-        c_scales = keep.tile([P, T - 1, PASSES, P], U8, align_bytes=64)
+        e_words = keep.tile([P, N_SLICES, PASSES, P], U32, align_bytes=64)
+        e_scales = keep.tile([P, N_SLICES, PASSES, P], U8, align_bytes=64)
+        c_words = keep.tile([P, N_SLICES, PASSES, P], U32, align_bytes=64)
+        c_scales = keep.tile([P, N_SLICES, PASSES, P], U8, align_bytes=64)
         xw_words = keep.tile([P, N_PAIRS, PASSES, P], U32, align_bytes=64)
         xw_scales = keep.tile([P, N_PAIRS, PASSES, P], U8, align_bytes=64)
         neg_max = keep.tile([P, N_PAIRS], F32)
@@ -78,23 +70,13 @@ def tile_infonceloss_pa_e_kernel(tc, embeddings, contexts, W_words, W_scales, ou
 
         nc.vector.memset(w_planes[:].bitcast(I32), 0)
 
-        def load_embeddings(lo, hi):
-            nc.sync.dma_start(out=e_raw[:, lo - 1 : hi - 1, :], in_=embeddings[:, lo:hi, :])
-
-        def load_contexts(lo, hi):
+        def load_slices(lo, hi):
+            nc.sync.dma_start(out=e_raw[:, lo:hi, :], in_=embeddings[:, 1 + lo : 1 + hi, :])
             nc.sync.dma_start(out=c_raw[:, lo:hi, :], in_=contexts[:, lo:hi, :])
 
-        def load_weight(step):
-            nc.sync.dma_start(
-                out=w_words[:, step, :, :].bitcast(I32),
-                in_=W_words[PASSES * step : PASSES * (step + 1)]
-                .rearrange("g p n t -> p g (n t)")
-                .bitcast(I32),
-            )
-
         def load_scale_slot(slot):
-            lo = PLANES_PER_TILE * slot
-            hi = min(lo + PLANES_PER_TILE, n_planes)
+            lo = PLANES_PER_SLOT * slot
+            hi = min(lo + PLANES_PER_SLOT, n_planes)
             for quadrant in range(P // QUADRANT):
                 top = QUADRANT * quadrant
                 nc.sync.dma_start(
@@ -102,17 +84,23 @@ def tile_infonceloss_pa_e_kernel(tc, embeddings, contexts, W_words, W_scales, ou
                     in_=W_scales[lo:hi, 4 * quadrant : 4 * quadrant + 4, :].bitcast(I32),
                 )
 
-        load_embeddings(1 + second_step, T)
-        load_scale_slot(PASSES * first_step // PLANES_PER_TILE)
-        load_weight(first_step)
-        load_contexts(0, times_of(first_step))
-        for slot in reversed(range(PASSES * first_step // PLANES_PER_TILE)):
+        def load_weight(step, lo, hi):
+            nc.sync.dma_start(
+                out=w_words[:, step, :, lo:hi].bitcast(I32),
+                in_=W_words[PASSES * step : PASSES * (step + 1)]
+                .rearrange("g p n t -> p g (n t)")[:, :, PACK * lo : PACK * hi]
+                .bitcast(I32),
+            )
+
+        load_slices(0, SLICES_PER_LOAD)
+        for slot in range(n_slots):
             load_scale_slot(slot)
-        load_weight(second_step)
-        load_contexts(times_of(first_step), T - 1)
-        load_embeddings(1, 1 + second_step)
-        for step in step_order[2:]:
-            load_weight(step)
+        for lo in range(SLICES_PER_LOAD, N_SLICES, SLICES_PER_LOAD):
+            load_slices(lo, min(lo + SLICES_PER_LOAD, N_SLICES))
+        load_weight(0, 0, K_PASS)
+        load_weight(0, K_PASS, D)
+        for step in range(1, STEPS):
+            load_weight(step, 0, D)
 
         ident_f32 = keep.tile([P, P], F32)
         make_identity(nc, ident_f32[:])
@@ -134,10 +122,10 @@ def tile_infonceloss_pa_e_kernel(tc, embeddings, contexts, W_words, W_scales, ou
             op=ALU.add,
         )
 
-        def turn_embedding_slice(te):
-            pairs_of_d = e_raw[:, te - 1, :].bitcast(F32)
+        def turn_embedding_slice(n):
+            pairs_of_d = e_raw[:, n, :].bitcast(F32)
             words_per_pass = K_PASS // 2
-            turned = psum_turned.tile([P, PASSES, 2, P], F32, tag="turned")
+            turned = psum_banks.tile([P, PASSES, 2, P], F32, tag="bank")
             for g in range(PASSES):
                 for u in range(2):
                     nc.tensor.transpose(
@@ -149,13 +137,13 @@ def tile_infonceloss_pa_e_kernel(tc, embeddings, contexts, W_words, W_scales, ou
             nc.scalar.copy(out=grouped[:].bitcast(F32), in_=turned[:].rearrange("p g u b -> p g b u"))
             return grouped
 
-        def turn_context_slice(s):
+        def turn_context_slice(n):
             grouped = slice_stage.tile([P, PASSES, P, PACK], BF16, tag="grouped", align_bytes=64)
             for g in range(PASSES):
-                turned = psum_turned.tile([P, PACK, P], BF16, tag="turned")
+                turned = psum_banks.tile([P, PACK, P], BF16, tag="bank")
                 for t in range(PACK):
                     lo = K_PASS * g + P * t
-                    nc.tensor.transpose(turned[:, t, :], c_raw[:, s, lo : lo + P], ident_bf16[:])
+                    nc.tensor.transpose(turned[:, t, :], c_raw[:, n, lo : lo + P], ident_bf16[:])
                 copy_out = nc.scalar.copy if g == 0 else nc.vector.tensor_copy
                 copy_out(out=grouped[:, g, :, :], in_=turned[:].rearrange("p t j -> p j t"))
             return grouped
@@ -167,29 +155,30 @@ def tile_infonceloss_pa_e_kernel(tc, embeddings, contexts, W_words, W_scales, ou
                 in_=grouped[:].rearrange("p g b t -> p (g b t)"),
             )
 
-        def quantise_embedding_slice(te, grouped):
-            quantise(grouped, e_words[:, te - 1, :, :], e_scales[:, te - 1, :, :])
-
-        def quantise_context_slice(s, grouped):
-            quantise(grouped, c_words[:, s, :, :], c_scales[:, s, :, :])
+        staged = {}
+        for n in range(N_SLICES + 1):
+            if n < N_SLICES:
+                staged[n] = (turn_embedding_slice(n), turn_context_slice(n))
+            if n >= 1:
+                grouped_e, grouped_c = staged[n - 1]
+                quantise(grouped_e, e_words[:, n - 1, :, :], e_scales[:, n - 1, :, :])
+                quantise(grouped_c, c_words[:, n - 1, :, :], c_scales[:, n - 1, :, :])
 
         def project(i):
             step, s = pairs[i]
-            te = 1 + step + s
             grouped = xw_stage.tile([P, PASSES, P, PACK], BF16, tag="xw_grouped", align_bytes=64)
             for g in range(PASSES):
-                bank = psum_xw.tile([P, PACK, P], F32, tag="xw_bank")
+                bank = psum_banks.tile([P, PACK, P], F32, tag="bank")
                 for t in range(PACK):
                     lo = K_PASS * g + P * t
                     for k_pass in range(PASSES):
-                        plane = PASSES * step + k_pass
-                        slot, place = divmod(plane, PLANES_PER_TILE)
+                        slot, place = divmod(PASSES * step + k_pass, PLANES_PER_SLOT)
                         nc.tensor.matmul_mx(
                             out=bank[:, t, :],
                             lhsT=w_words[:, step, k_pass, lo : lo + P].bitcast(FP8X4),
                             lhsT_scale=w_planes[4 * place : P, slot, lo : lo + P],
-                            rhs=e_words[:, te - 1, k_pass, :].bitcast(FP8X4),
-                            rhs_scale=e_scales[:, te - 1, k_pass, :],
+                            rhs=e_words[:, step + s, k_pass, :].bitcast(FP8X4),
+                            rhs_scale=e_scales[:, step + s, k_pass, :],
                             start=(k_pass == 0),
                             stop=(k_pass == PASSES - 1),
                         )
@@ -200,7 +189,6 @@ def tile_infonceloss_pa_e_kernel(tc, embeddings, contexts, W_words, W_scales, ou
 
         def compare(i):
             step, s = pairs[i]
-            column = first_column(step) + s
             scores = psum_scores.tile([P, P], F32, tag="scores")
             for g in range(PASSES):
                 nc.tensor.matmul_mx(
@@ -212,27 +200,7 @@ def tile_infonceloss_pa_e_kernel(tc, embeddings, contexts, W_words, W_scales, ou
                     start=(g == 0),
                     stop=(g == PASSES - 1),
                 )
-            nc.vector.tensor_reduce(
-                out=neg_max[:, column : column + 1], in_=scores[:], axis=AXIS_X, op=ALU.max, negate=True
-            )
-            return scores
-
-        def sum_exponentials(i, scores):
-            step, s = pairs[i]
-            column = first_column(step) + s
-            exponentials = unread.tile([P, P], F32, tag="exponentials")
-            nc.scalar.activation(
-                out=exponentials[:],
-                in_=scores[:],
-                func=ACT.Exp,
-                bias=neg_max[:, column : column + 1],
-                scale=1.0,
-                accum_out=sum_exp[:, column : column + 1],
-            )
-
-        def take_diagonal(i, scores):
-            step, s = pairs[i]
-            column = first_column(step) + s
+            nc.vector.tensor_reduce(out=neg_max[:, i : i + 1], in_=scores[:], axis=AXIS_X, op=ALU.max, negate=True)
             masked = unread.tile([P, P], F32, tag="masked")
             nc.vector.scalar_tensor_tensor(
                 out=masked[:],
@@ -241,12 +209,24 @@ def tile_infonceloss_pa_e_kernel(tc, embeddings, contexts, W_words, W_scales, ou
                 in1=ident_f32[:],
                 op0=ALU.mult,
                 op1=ALU.mult,
-                accum_out=diagonal[:, column : column + 1],
+                accum_out=diagonal[:, i : i + 1],
+            )
+            return scores
+
+        def sum_exponentials(i, scores):
+            exponentials = unread.tile([P, P], F32, tag="exponentials")
+            nc.scalar.activation(
+                out=exponentials[:],
+                in_=scores[:],
+                func=ACT.Exp,
+                bias=neg_max[:, i : i + 1],
+                scale=1.0,
+                accum_out=sum_exp[:, i : i + 1],
             )
 
         def spread(step, values, spread_tile):
-            n_times = times_of(step)
-            lo = first_column(step)
+            n_times = N_SLICES - step
+            lo = first_pair[step]
             shape = [P, ROWS_PER_GROUP, n_times]
             nc.vector.tensor_tensor(
                 out=spread_tile[:, ROWS_PER_GROUP * lo : ROWS_PER_GROUP * (lo + n_times)].rearrange(
@@ -258,8 +238,8 @@ def tile_infonceloss_pa_e_kernel(tc, embeddings, contexts, W_words, W_scales, ou
             )
 
         def spread_shift_of(step):
-            n_times = times_of(step)
-            lo = first_column(step)
+            n_times = N_SLICES - step
+            lo = first_pair[step]
             nc.vector.scalar_tensor_tensor(
                 out=shift[:, lo : lo + n_times],
                 in0=neg_max[:, lo : lo + n_times],
@@ -270,19 +250,9 @@ def tile_infonceloss_pa_e_kernel(tc, embeddings, contexts, W_words, W_scales, ou
             )
             spread(step, shift, spread_shift)
 
-        early_times = list(range(1 + second_step, T))
-        early_grouped = [turn_embedding_slice(te) for te in early_times]
-        for te, grouped in zip(early_times, early_grouped):
-            quantise_embedding_slice(te, grouped)
-        later_slices = [("contexts", s) for s in range(times_of(first_step))]
-        for step in step_order[1:]:
-            later_slices.append(("contexts", times_of(step) - 1))
-            if step >= 1:
-                later_slices.append(("embeddings", step))
-
         def ends_step(i):
             step, s = pairs[i]
-            return s == times_of(step) - 1
+            return s == N_SLICES - step - 1
 
         grouped_of = {}
         scores_of = {}
@@ -291,16 +261,8 @@ def tile_infonceloss_pa_e_kernel(tc, embeddings, contexts, W_words, W_scales, ou
                 sum_exponentials(i - EXP_LAG, scores_of[i - EXP_LAG])
                 if ends_step(i - EXP_LAG):
                     spread(pairs[i - EXP_LAG][0], sum_exp, spread_sum)
-            turns_slice = 1 <= i <= len(later_slices)
-            if turns_slice:
-                kind, time = later_slices[i - 1]
-                if kind == "contexts":
-                    slice_grouped = turn_context_slice(time)
-                else:
-                    slice_grouped = turn_embedding_slice(time)
             if 0 <= i - COMPARE_LAG < N_PAIRS:
                 scores_of[i - COMPARE_LAG] = compare(i - COMPARE_LAG)
-                take_diagonal(i - COMPARE_LAG, scores_of[i - COMPARE_LAG])
                 if ends_step(i - COMPARE_LAG):
                     spread_shift_of(pairs[i - COMPARE_LAG][0])
             if 0 <= i - QUANTISE_LAG < N_PAIRS:
@@ -309,25 +271,20 @@ def tile_infonceloss_pa_e_kernel(tc, embeddings, contexts, W_words, W_scales, ou
                     xw_words[:, i - QUANTISE_LAG, :, :],
                     xw_scales[:, i - QUANTISE_LAG, :, :],
                 )
-            if turns_slice:
-                if kind == "contexts":
-                    quantise_context_slice(time, slice_grouped)
-                else:
-                    quantise_embedding_slice(time, slice_grouped)
             if i < N_PAIRS:
                 grouped_of[i] = project(i)
 
-        gathered_sum = psum_turned.tile([P, ROWS_PER_GROUP * N_PAIRS], F32, tag="turned")
-        nc.tensor.matmul(out=gathered_sum[:], lhsT=group_of_row[:], rhs=spread_sum[:], start=True, stop=True)
-        gathered_shift = psum_turned.tile([P, ROWS_PER_GROUP * N_PAIRS], F32, tag="turned")
+        gathered_shift = psum_banks.tile([P, ROWS_PER_GROUP * N_PAIRS], F32, tag="bank")
         nc.tensor.matmul(out=gathered_shift[:], lhsT=group_of_row[:], rhs=spread_shift[:], start=True, stop=True)
+        gathered_sum = psum_banks.tile([P, ROWS_PER_GROUP * N_PAIRS], F32, tag="bank")
+        nc.tensor.matmul(out=gathered_sum[:], lhsT=group_of_row[:], rhs=spread_sum[:], start=True, stop=True)
         log_sum = keep.tile([GROUPS, ROWS_PER_GROUP * N_PAIRS], F32)
         nc.scalar.activation(out=log_sum[:], in_=gathered_sum[0:GROUPS, :], func=ACT.Ln)
         loss = keep.tile([GROUPS, ROWS_PER_GROUP * N_PAIRS], F32)
         nc.vector.tensor_tensor(out=loss[:], in0=log_sum[:], in1=gathered_shift[0:GROUPS, :], op=ALU.subtract)
         for step in range(STEPS):
-            lo = first_column(step)
-            hi = lo + times_of(step)
+            lo = first_pair[step]
+            hi = lo + N_SLICES - step
             nc.sync.dma_start(
                 out=out[P * lo : P * hi].rearrange("(q r) -> q r", q=GROUPS),
                 in_=loss[:, ROWS_PER_GROUP * lo : ROWS_PER_GROUP * hi],

@@ -140,10 +140,12 @@ def tile_infonceloss_pa_e_kernel(tc, embeddings, contexts, W_words, W_scales, ou
         def turn_context_slice(n):
             grouped = slice_stage.tile([P, PASSES, P, PACK], BF16, tag="grouped", align_bytes=64)
             for g in range(PASSES):
-                turned = psum_banks.tile([P, PACK, P], BF16, tag="bank")
+                turned = psum_banks.tile([P, PACK, P], F32, tag="bank")
                 for t in range(PACK):
                     lo = K_PASS * g + P * t
-                    nc.tensor.transpose(turned[:, t, :], c_raw[:, n, lo : lo + P], ident_bf16[:])
+                    nc.tensor.matmul(
+                        out=turned[:, t, :], lhsT=c_raw[:, n, lo : lo + P], rhs=ident_bf16[:], start=True, stop=True
+                    )
                 copy_out = nc.scalar.copy if g == 0 else nc.vector.tensor_copy
                 copy_out(out=grouped[:, g, :, :], in_=turned[:].rearrange("p t j -> p j t"))
             return grouped

import math
from contextlib import ExitStack

import concourse.mybir as mybir
from concourse.masks import make_identity

F32 = mybir.dt.float32
BF16 = mybir.dt.bfloat16
I32 = mybir.dt.int32
U32 = mybir.dt.uint32
U8 = mybir.dt.uint8
FP8X4 = mybir.dt.float8_e4m3fn_x4
ALU = mybir.AluOpType
ACT = mybir.ActivationFunctionType
AXIS_X = mybir.AxisListType.X

P = 128
T = 8
N_SLICES = T - 1
D = 1024
STEPS = 5
PACK = 4
K_PASS = P * PACK
PASSES = D // K_PASS
PLANES_PER_SLOT = 4
QUADRANT = 32
SLICES_PER_LOAD = 2
ROWS_PER_GROUP = 8
GROUPS = P // ROWS_PER_GROUP
QUANTISE_LAG = 1
COMPARE_LAG = 3
EXP_LAG = 4

N_PAIRS = sum(N_SLICES - step for step in range(STEPS))
FLOPS = 2 * N_PAIRS * P * D * D + 2 * N_PAIRS * P * P * D


def tile_infonceloss_pa_e_kernel(tc, embeddings, contexts, W_words, W_scales, out):
    nc = tc.nc
    pairs = [(step, s) for step in range(STEPS) for s in range(N_SLICES - step)]
    first_pair = [pairs.index((step, 0)) for step in range(STEPS)]

    with ExitStack() as ctx:
        keep = ctx.enter_context(tc.tile_pool(name="keep", bufs=1))
        slice_stage = ctx.enter_context(tc.tile_pool(name="slice_stage", bufs=4))
        xw_stage = ctx.enter_context(tc.tile_pool(name="xw_stage", bufs=3))
        unread = ctx.enter_context(tc.tile_pool(name="unread", bufs=4))
        psum_banks = ctx.enter_context(tc.psum_pool(name="psum_banks", bufs=6))
        psum_scores = ctx.enter_context(tc.psum_pool(name="psum_scores", bufs=2))
        ctx.enter_context(tc.manual_schedule())

        e_raw = keep.tile([P, N_SLICES, D], BF16)
        c_raw = keep.tile([P, N_SLICES, D], BF16)
        w_words = keep.tile([P, STEPS, PASSES, D], U32, align_bytes=64)
        n_planes = STEPS * PASSES
        n_slots = (n_planes + PLANES_PER_SLOT - 1) // PLANES_PER_SLOT
        w_planes = keep.tile([P, n_slots, D], U8, align_bytes=64)
        e_words = keep.tile([P, N_SLICES, PASSES, P], U32, align_bytes=64)
        e_scales = keep.tile([P, N_SLICES, PASSES, P], U8, align_bytes=64)
        c_words = keep.tile([P, N_SLICES, PASSES, P], U32, align_bytes=64)
        c_scales = keep.tile([P, N_SLICES, PASSES, P], U8, align_bytes=64)
        xw_words = keep.tile([P, N_PAIRS, PASSES, P], U32, align_bytes=64)
        xw_scales = keep.tile([P, N_PAIRS, PASSES, P], U8, align_bytes=64)
        neg_max = keep.tile([P, N_PAIRS], F32)
        sum_exp = keep.tile([P, N_PAIRS], F32)
        diagonal = keep.tile([P, N_PAIRS], F32)
        shift = keep.tile([P, N_PAIRS], F32)
        spread_sum = keep.tile([P, ROWS_PER_GROUP * N_PAIRS], F32)
        spread_shift = keep.tile([P, ROWS_PER_GROUP * N_PAIRS], F32)

        nc.vector.memset(w_planes[:].bitcast(I32), 0)

        def load_slices(lo, hi):
            nc.sync.dma_start(out=e_raw[:, lo:hi, :], in_=embeddings[:, 1 + lo : 1 + hi, :])
            nc.sync.dma_start(out=c_raw[:, lo:hi, :], in_=contexts[:, lo:hi, :])

        def load_scale_slot(slot):
            lo = PLANES_PER_SLOT * slot
            hi = min(lo + PLANES_PER_SLOT, n_planes)
            for quadrant in range(P // QUADRANT):
                top = QUADRANT * quadrant
                nc.sync.dma_start(
                    out=w_planes[top : top + 4 * (hi - lo), slot, :].bitcast(I32),
                    in_=W_scales[lo:hi, 4 * quadrant : 4 * quadrant + 4, :].bitcast(I32),
                )

        def load_weight(step, lo, hi):
            nc.sync.dma_start(
                out=w_words[:, step, :, lo:hi].bitcast(I32),
                in_=W_words[PASSES * step : PASSES * (step + 1)]
                .rearrange("g p n t -> p g (n t)")[:, :, PACK * lo : PACK * hi]
                .bitcast(I32),
            )

        load_slices(0, SLICES_PER_LOAD)
        for slot in range(n_slots):
            load_scale_slot(slot)
        for lo in range(SLICES_PER_LOAD, N_SLICES, SLICES_PER_LOAD):
            load_slices(lo, min(lo + SLICES_PER_LOAD, N_SLICES))
        load_weight(0, 0, K_PASS)
        load_weight(0, K_PASS, D)
        for step in range(1, STEPS):
            load_weight(step, 0, D)

        ident_f32 = keep.tile([P, P], F32)
        make_identity(nc, ident_f32[:])
        ident_bf16 = keep.tile([P, P], BF16)
        make_identity(nc, ident_bf16[:])
        group_of_row = keep.tile([P, P], F32)
        nc.vector.memset(group_of_row[:], 0.0)
        nc.vector.tensor_reduce(
            out=group_of_row[:, 0:GROUPS],
            in_=ident_f32[:].rearrange("p (q i) -> p q i", i=ROWS_PER_GROUP),
            axis=AXIS_X,
            op=ALU.add,
        )
        place_in_group = keep.tile([P, ROWS_PER_GROUP], F32)
        nc.vector.tensor_reduce(
            out=place_in_group[:],
            in_=ident_f32[:].rearrange("p (q i) -> p i q", i=ROWS_PER_GROUP),
            axis=AXIS_X,
            op=ALU.add,
        )

        def turn_embedding_slice(n):
            pairs_of_d = e_raw[:, n, :].bitcast(F32)
            words_per_pass = K_PASS // 2
            turned = psum_banks.tile([P, PASSES, 2, P], F32, tag="bank")
            for g in range(PASSES):
                for u in range(2):
                    nc.tensor.transpose(
                        turned[:, g, u, :],
                        pairs_of_d[:, words_per_pass * g + u : words_per_pass * (g + 1) : 2],
                        ident_f32[:],
                    )
            grouped = slice_stage.tile([P, PASSES, P, PACK], BF16, tag="grouped", align_bytes=64)
            nc.scalar.copy(out=grouped[:].bitcast(F32), in_=turned[:].rearrange("p g u b -> p g b u"))
            return grouped

        def turn_context_slice(n):
            grouped = slice_stage.tile([P, PASSES, P, PACK], BF16, tag="grouped", align_bytes=64)
            for g in range(PASSES):
                turned = psum_banks.tile([P, PACK, P], F32, tag="bank")
                for t in range(PACK):
                    lo = K_PASS * g + P * t
                    nc.tensor.matmul(
                        out=turned[:, t, :], lhsT=c_raw[:, n, lo : lo + P], rhs=ident_bf16[:], start=True, stop=True
                    )
                copy_out = nc.scalar.copy if g == 0 else nc.vector.tensor_copy
                copy_out(out=grouped[:, g, :, :], in_=turned[:].rearrange("p t j -> p j t"))
            return grouped

        def quantise(grouped, words, scales):
            nc.vector.quantize_mx(
                out=words.rearrange("p g b -> p (g b)").bitcast(FP8X4),
                scales=scales.rearrange("p g b -> p (g b)"),
                in_=grouped[:].rearrange("p g b t -> p (g b t)"),
            )

        staged = {}
        for n in range(N_SLICES + 1):
            if n < N_SLICES:
                staged[n] = (turn_embedding_slice(n), turn_context_slice(n))
            if n >= 1:
                grouped_e, grouped_c = staged[n - 1]
                quantise(grouped_e, e_words[:, n - 1, :, :], e_scales[:, n - 1, :, :])
                quantise(grouped_c, c_words[:, n - 1, :, :], c_scales[:, n - 1, :, :])

        def project(i):
            step, s = pairs[i]
            grouped = xw_stage.tile([P, PASSES, P, PACK], BF16, tag="xw_grouped", align_bytes=64)
            for g in range(PASSES):
                bank = psum_banks.tile([P, PACK, P], F32, tag="bank")
                for t in range(PACK):
                    lo = K_PASS * g + P * t
                    for k_pass in range(PASSES):
                        slot, place = divmod(PASSES * step + k_pass, PLANES_PER_SLOT)
                        nc.tensor.matmul_mx(
                            out=bank[:, t, :],
                            lhsT=w_words[:, step, k_pass, lo : lo + P].bitcast(FP8X4),
                            lhsT_scale=w_planes[4 * place : P, slot, lo : lo + P],
                            rhs=e_words[:, step + s, k_pass, :].bitcast(FP8X4),
                            rhs_scale=e_scales[:, step + s, k_pass, :],
                            start=(k_pass == 0),
                            stop=(k_pass == PASSES - 1),
                        )
                to_vector = i % 2 == 1 and g == PASSES - 1
                copy_out = nc.vector.tensor_copy if to_vector else nc.scalar.copy
                copy_out(out=grouped[:, g, :, :], in_=bank[:].rearrange("p t b -> p b t"))
            return grouped

        def compare(i):
            step, s = pairs[i]
            scores = psum_scores.tile([P, P], F32, tag="scores")
            for g in range(PASSES):
                nc.tensor.matmul_mx(
                    out=scores[:],
                    lhsT=xw_words[:, i, g, :].bitcast(FP8X4),
                    lhsT_scale=xw_scales[:, i, g, :],
                    rhs=c_words[:, s, g, :].bitcast(FP8X4),
                    rhs_scale=c_scales[:, s, g, :],
                    start=(g == 0),
                    stop=(g == PASSES - 1),
                )
            nc.vector.tensor_reduce(out=neg_max[:, i : i + 1], in_=scores[:], axis=AXIS_X, op=ALU.max, negate=True)
            masked = unread.tile([P, P], F32, tag="masked")
            nc.vector.scalar_tensor_tensor(
                out=masked[:],
                in0=scores[:],
                scalar=1.0,
                in1=ident_f32[:],
                op0=ALU.mult,
                op1=ALU.mult,
                accum_out=diagonal[:, i : i + 1],
            )
            return scores

        def sum_exponentials(i, scores):
            exponentials = unread.tile([P, P], F32, tag="exponentials")
            nc.scalar.activation(
                out=exponentials[:],
                in_=scores[:],
                func=ACT.Exp,
                bias=neg_max[:, i : i + 1],
                scale=1.0,
                accum_out=sum_exp[:, i : i + 1],
            )

        def spread(step, values, spread_tile):
            n_times = N_SLICES - step
            lo = first_pair[step]
            shape = [P, ROWS_PER_GROUP, n_times]
            nc.vector.tensor_tensor(
                out=spread_tile[:, ROWS_PER_GROUP * lo : ROWS_PER_GROUP * (lo + n_times)].rearrange(
                    "p (i s) -> p i s", s=n_times
                ),
                in0=values[:, lo : lo + n_times].unsqueeze(1).to_broadcast(shape),
                in1=place_in_group[:].unsqueeze(2).to_broadcast(shape),
                op=ALU.mult,
            )

        def spread_shift_of(step):
            n_times = N_SLICES - step
            lo = first_pair[step]
            nc.vector.scalar_tensor_tensor(
                out=shift[:, lo : lo + n_times],
                in0=neg_max[:, lo : lo + n_times],
                scalar=math.log(P * n_times),
                in1=diagonal[:, lo : lo + n_times],
                op0=ALU.add,
                op1=ALU.add,
            )
            spread(step, shift, spread_shift)

        def ends_step(i):
            step, s = pairs[i]
            return s == N_SLICES - step - 1

        grouped_of = {}
        scores_of = {}
        for i in range(N_PAIRS + EXP_LAG):
            if 0 <= i - EXP_LAG:
                sum_exponentials(i - EXP_LAG, scores_of[i - EXP_LAG])
                if ends_step(i - EXP_LAG):
                    spread(pairs[i - EXP_LAG][0], sum_exp, spread_sum)
            if 0 <= i - COMPARE_LAG < N_PAIRS:
                scores_of[i - COMPARE_LAG] = compare(i - COMPARE_LAG)
                if ends_step(i - COMPARE_LAG):
                    spread_shift_of(pairs[i - COMPARE_LAG][0])
            if 0 <= i - QUANTISE_LAG < N_PAIRS:
                quantise(
                    grouped_of[i - QUANTISE_LAG],
                    xw_words[:, i - QUANTISE_LAG, :, :],
                    xw_scales[:, i - QUANTISE_LAG, :, :],
                )
            if i < N_PAIRS:
                grouped_of[i] = project(i)

        gathered_shift = psum_banks.tile([P, ROWS_PER_GROUP * N_PAIRS], F32, tag="bank")
        nc.tensor.matmul(out=gathered_shift[:], lhsT=group_of_row[:], rhs=spread_shift[:], start=True, stop=True)
        gathered_sum = psum_banks.tile([P, ROWS_PER_GROUP * N_PAIRS], F32, tag="bank")
        nc.tensor.matmul(out=gathered_sum[:], lhsT=group_of_row[:], rhs=spread_sum[:], start=True, stop=True)
        log_sum = keep.tile([GROUPS, ROWS_PER_GROUP * N_PAIRS], F32)
        nc.scalar.activation(out=log_sum[:], in_=gathered_sum[0:GROUPS, :], func=ACT.Ln)
        loss = keep.tile([GROUPS, ROWS_PER_GROUP * N_PAIRS], F32)
        nc.vector.tensor_tensor(out=loss[:], in0=log_sum[:], in1=gathered_shift[0:GROUPS, :], op=ALU.subtract)
        for step in range(STEPS):
            lo = first_pair[step]
            hi = lo + N_SLICES - step
            nc.sync.dma_start(
                out=out[P * lo : P * hi].rearrange("(q r) -> q r", q=GROUPS),
                in_=loss[:, ROWS_PER_GROUP * lo : ROWS_PER_GROUP * hi],
            )
